import numpy as np
import ml_dtypes


def mxq(x, axis, fmt="e4m3"):
    dtype, down = {"e4m3": (ml_dtypes.float8_e4m3fn, 7), "e5m2": (ml_dtypes.float8_e5m2, 14)}[fmt]
    v = np.moveaxis(np.asarray(x, np.float32).astype(ml_dtypes.bfloat16).astype(np.float64), axis, -1)
    blocks = v.reshape(v.shape[:-1] + (-1, 32))
    amax = np.abs(blocks).max(-1, keepdims=True)
    byte = np.maximum(np.where(amax > 0, np.frexp(amax)[1] - 1 + 127, 0) - down, 1)
    scale = np.exp2(byte - 127.0)
    codes = (blocks / scale).astype(np.float32).astype(dtype).astype(np.float64)
    return np.moveaxis((codes * scale).reshape(v.shape), -1, axis)


WIDE = False


def mx_kscale(k):
    if not WIDE:
        return np.ones(k)
    levels = np.array([10, -10, 5, -5, 0])
    a = np.random.permutation(np.resize(levels, k // 512 * 4)).reshape(k // 512, 4)
    idx = np.arange(k)
    return np.exp2(a[idx // 512, idx % 128 // 32])


BF16 = ml_dtypes.bfloat16


def bf(x):
    return np.asarray(x, np.float32).astype(BF16)


def f64(x):
    return np.asarray(x).astype(np.float64)


B, HC, WC, C, F = 128, 2, 2, 8192, 128


def setup_inputs():
    s = mx_kscale(C)
    x_crop = np.stack([np.random.standard_normal((B, HC, WC, C)), np.random.standard_normal((B, HC, WC, C))], axis=1)
    return {"x_crop": bf(x_crop * s),
            "W_r": bf(np.random.standard_normal((HC, WC, C, F)) * 0.5 / np.sqrt(C) / s[:, None]),
            "W_i": bf(np.random.standard_normal((HC, WC, C, F)) * 0.5 / np.sqrt(C) / s[:, None]),
            "b_r": bf(np.random.standard_normal(F) * 0.3),
            "b_i": bf(np.random.standard_normal(F) * 0.3)}


def reference(x_crop, W_r, W_i, b_r, b_i):
    sp = f64(x_crop)
    xr = mxq(sp[:, 0].transpose(1, 2, 0, 3), 3, "e4m3")
    xi = mxq(sp[:, 1].transpose(1, 2, 0, 3), 3, "e4m3")
    wr = mxq(f64(W_r), 2, "e4m3")
    wi = mxq(f64(W_i), 2, "e4m3")
    rr = xr @ wr
    ii = xi @ wi
    ri = xr @ wi
    ir = xi @ wr
    r = rr - ii + f64(b_r)
    i = ri + ir + f64(b_i)
    y = np.stack([r.transpose(2, 0, 1, 3), i.transpose(2, 0, 1, 3)], axis=1)
    return np.maximum(y, 0.0)

@@ -1,0 +1,206 @@
+from contextlib import ExitStack
+
+import concourse.mybir as mybir
+from concourse.masks import make_identity
+
+BF16 = mybir.dt.bfloat16
+F32 = mybir.dt.float32
+U32 = mybir.dt.uint32
+U8 = mybir.dt.uint8
+FP8X4 = mybir.dt.float8_e4m3fn_x4
+
+P = 128
+PACK = 4
+K_PASS = P * PACK
+
+BATCH = 128
+PIXEL_COLS = 2
+PIXELS = 4
+CHANNELS = 8192
+FEATURES = 128
+REAL, IMAG = 0, 1
+
+PASSES = 4
+K_CHUNK = PASSES * K_PASS
+CHUNKS_PER_PIXEL = CHANNELS // K_CHUNK
+CHUNKS = PIXELS * CHUNKS_PER_PIXEL
+HALF = PASSES // 2
+
+X_COLS = BATCH
+W_COLS = 2 * FEATURES
+
+RAW_BUFS = 6
+
+FLOPS = 4 * PIXELS * 2 * BATCH * CHANNELS * FEATURES
+
+
+def tile_dot_pa_k_kernel(tc, x_crop, W_r, W_i, b_r, b_i, out):
+    nc = tc.nc
+    with ExitStack() as ctx:
+        const = ctx.enter_context(tc.tile_pool(name="const", bufs=1))
+        raw = ctx.enter_context(tc.tile_pool(name="raw", bufs=RAW_BUFS))
+        work = ctx.enter_context(tc.tile_pool(name="work", bufs=2))
+        psum_t = ctx.enter_context(tc.psum_pool(name="psum_t", bufs=4))
+        psum_acc = ctx.enter_context(tc.psum_pool(name="psum_acc", bufs=2))
+        ctx.enter_context(tc.manual_schedule())
+
+        x_raw, w_raw = {}, {}
+        x_codes, x_scales = {}, {}
+        w_codes, w_scales = {}, {}
+        sums = {}
+
+        def place(n):
+            pixel, quarter = divmod(n, CHUNKS_PER_PIXEL)
+            h, w = divmod(pixel, PIXEL_COLS)
+            return h, w, slice(quarter * K_CHUNK, (quarter + 1) * K_CHUNK)
+
+        def load_x(n):
+            h, w, channels = place(n)
+            x_raw[n] = raw.tile([P, 2, K_CHUNK], BF16, name="x_raw", tag="x_raw")
+            nc.sync.dma_start(out=x_raw[n][:], in_=x_crop[:, :, h, w, channels])
+
+        def load_w(n):
+            h, w, channels = place(n)
+            w_raw[n] = raw.tile([P, 2, PASSES, PACK * FEATURES], BF16, name="w_raw", tag="w_raw")
+            for part, weights in ((REAL, W_r), (IMAG, W_i)):
+                nc.sync.dma_start(
+                    out=w_raw[n][:, part],
+                    in_=weights[h, w, channels, :].rearrange("(c p j) f -> p c (j f)", p=P, j=PACK),
+                )
+
+        def transpose_x(n):
+            x_grouped = work.tile([P, 2 * PASSES * X_COLS * PACK], BF16, align_bytes=64)
+            bank_cols = HALF * X_COLS * PACK
+            for part in (REAL, IMAG):
+                words = x_raw[n][:, part, :].bitcast(F32)
+                words = words.rearrange("b (c p u) -> b c u p", p=P, u=2)
+                for half in range(2):
+                    bank = psum_t.tile([P, HALF, 2, BATCH], F32, name="bank", tag="bank")
+                    for c in range(HALF):
+                        for u in range(2):
+                            nc.tensor.transpose(
+                                bank[:, c, u, :], words[:, half * HALF + c, u, :], identity[:]
+                            )
+                    start = (part * 2 + half) * bank_cols
+                    pairs = x_grouped[:, start : start + bank_cols].bitcast(F32)
+                    nc.scalar.copy(
+                        out=pairs.rearrange("p (c b u) -> p c b u", c=HALF, u=2),
+                        in_=bank[:].rearrange("p c u b -> p c b u"),
+                    )
+            return x_grouped
+
+        def quantise_x(n, x_grouped):
+            x_codes[n] = work.tile([P, 2 * PASSES * X_COLS], U32, name="x_codes", align_bytes=64)
+            x_scales[n] = work.tile([P, 2 * PASSES * X_COLS], U8, name="x_scales", align_bytes=64)
+            nc.vector.quantize_mx(
+                out=x_codes[n][:].bitcast(FP8X4), scales=x_scales[n][:], in_=x_grouped[:]
+            )
+
+        def regroup_w(n):
+            w_grouped = work.tile([P, PASSES, 2, FEATURES, PACK], BF16, align_bytes=64)
+
+            def views(part, passes):
+                src = w_raw[n][:, part, passes, :]
+                dst = w_grouped[:, passes, part, :, :]
+                return (
+                    dst.rearrange("p c (g i) j -> p c g j i", i=4),
+                    src.rearrange("p c (j g i) -> p c g j i", j=PACK, i=4),
+                )
+
+            first, second = slice(0, HALF), slice(HALF, PASSES)
+            for part, passes in ((REAL, first), (IMAG, first), (REAL, second)):
+                dst, src = views(part, passes)
+                nc.vector.tensor_copy(out=dst, in_=src)
+            for c in range(HALF, PASSES):
+                dst, src = views(IMAG, slice(c, c + 1))
+                nc.scalar.copy(out=dst[:, 0], in_=src[:, 0])
+            return w_grouped
+
+        def quantise_w(n, w_grouped):
+            w_codes[n] = work.tile([P, PASSES * W_COLS], U32, name="w_codes", align_bytes=64)
+            w_scales[n] = work.tile([P, PASSES * W_COLS], U8, name="w_scales", align_bytes=64)
+            for half in range(2):
+                cols = slice(half * HALF * W_COLS, (half + 1) * HALF * W_COLS)
+                passes = slice(half * HALF, (half + 1) * HALF)
+                nc.vector.quantize_mx(
+                    out=w_codes[n][:, cols].bitcast(FP8X4),
+                    scales=w_scales[n][:, cols],
+                    in_=w_grouped[:, passes].rearrange("p c z f j -> p (c z f j)"),
+                )
+
+        def multiply(n):
+            pixel, quarter = divmod(n, CHUNKS_PER_PIXEL)
+            if quarter == 0:
+                sums[pixel] = (
+                    psum_acc.tile([P, 2, FEATURES], F32, name="sum_xr", tag="sum_xr"),
+                    psum_acc.tile([P, 2, FEATURES], F32, name="sum_xi", tag="sum_xi"),
+                )
+            for half in range(2):
+                for part in (IMAG, REAL):
+                    for c in range(half * HALF, (half + 1) * HALF):
+                        x_cols = slice((part * PASSES + c) * X_COLS, (part * PASSES + c + 1) * X_COLS)
+                        w_cols = slice(c * W_COLS, (c + 1) * W_COLS)
+                        nc.tensor.matmul_mx(
+                            out=sums[pixel][part][:].rearrange("b z f -> b (z f)"),
+                            lhsT=x_codes[n][:, x_cols].bitcast(FP8X4),
+                            lhsT_scale=x_scales[n][:, x_cols],
+                            rhs=w_codes[n][:, w_cols].bitcast(FP8X4),
+                            rhs_scale=w_scales[n][:, w_cols],
+                            start=(quarter == 0 and c == 0),
+                            stop=(quarter == CHUNKS_PER_PIXEL - 1 and c == PASSES - 1),
+                        )
+
+        def finish_pixel(pixel):
+            h, w = divmod(pixel, PIXEL_COLS)
+            sum_xr, sum_xi = sums[pixel]
+            rest = work.tile([P, 2, FEATURES], F32)
+            result = work.tile([P, 2, FEATURES], F32)
+            nc.vector.tensor_sub(out=rest[:, REAL, :], in0=bias[:, REAL, :], in1=sum_xi[:, IMAG, :])
+            nc.vector.tensor_add(out=rest[:, IMAG, :], in0=bias[:, IMAG, :], in1=sum_xi[:, REAL, :])
+            nc.vector.tensor_add(out=result[:], in0=rest[:], in1=sum_xr[:])
+            nc.vector.tensor_scalar_max(out=result[:], in0=result[:], scalar1=0.0)
+            nc.sync.dma_start(out=out[:, :, h, w, :], in_=result[:])
+
+        load_x(0)
+        for n in range(RAW_BUFS - 1):
+            load_x(n + 1)
+            load_w(n)
+
+        identity = const.tile([P, P], F32)
+        make_identity(nc, identity[:])
+        ones = const.tile([P, P], BF16)
+        bias_row = const.tile([P, 2, FEATURES], BF16)
+        nc.vector.memset(ones[:], 1.0)
+        nc.vector.memset(bias_row[:], 0.0)
+        nc.scalar.dma_start(out=bias_row[0:1, REAL, :], in_=b_r.rearrange("(o f) -> o f", o=1))
+        nc.scalar.dma_start(out=bias_row[0:1, IMAG, :], in_=b_i.rearrange("(o f) -> o f", o=1))
+
+        x_grouped = transpose_x(0)
+        quantise_x(0, x_grouped)
+
+        bias_bank = psum_t.tile([P, 2, FEATURES], F32, name="bias_bank", tag="bank")
+        bias = const.tile([P, 2, FEATURES], F32)
+        nc.tensor.matmul(
+            out=bias_bank[:].rearrange("b z f -> b (z f)"),
+            lhsT=ones[:],
+            rhs=bias_row[:].rearrange("k z f -> k (z f)"),
+            start=True,
+            stop=True,
+        )
+        nc.scalar.copy(out=bias[:], in_=bias_bank[:])
+
+        for n in range(CHUNKS):
+            if n + RAW_BUFS < CHUNKS:
+                load_x(n + RAW_BUFS)
+            if n + RAW_BUFS - 1 < CHUNKS:
+                load_w(n + RAW_BUFS - 1)
+            if n + 1 < CHUNKS:
+                x_grouped = transpose_x(n + 1)
+            if n > 0 and n % CHUNKS_PER_PIXEL == 0:
+                finish_pixel(n // CHUNKS_PER_PIXEL - 1)
+            w_grouped = regroup_w(n)
+            if n + 1 < CHUNKS:
+                quantise_x(n + 1, x_grouped)
+            quantise_w(n, w_grouped)
+            multiply(n)
+        finish_pixel(PIXELS - 1)

@@ -30,6 +30,7 @@ X_COLS = BATCH
 W_COLS = 2 * FEATURES
 
 RAW_BUFS = 6
+X_AHEAD = 2
 
 FLOPS = 4 * PIXELS * 2 * BATCH * CHANNELS * FEATURES
 
@@ -45,6 +46,7 @@ def tile_dot_pa_k_kernel(tc, x_crop, W_r, W_i, b_r, b_i, out):
         ctx.enter_context(tc.manual_schedule())
 
         x_raw, w_raw = {}, {}
+        x_grouped = {}
         x_codes, x_scales = {}, {}
         w_codes, w_scales = {}, {}
         sums = {}
@@ -69,7 +71,9 @@ def tile_dot_pa_k_kernel(tc, x_crop, W_r, W_i, b_r, b_i, out):
                 )
 
         def transpose_x(n):
-            x_grouped = work.tile([P, 2 * PASSES * X_COLS * PACK], BF16, align_bytes=64)
+            x_grouped[n] = work.tile(
+                [P, 2 * PASSES * X_COLS * PACK], BF16, name="x_grouped", align_bytes=64
+            )
             bank_cols = HALF * X_COLS * PACK
             for part in (REAL, IMAG):
                 words = x_raw[n][:, part, :].bitcast(F32)
@@ -82,18 +86,17 @@ def tile_dot_pa_k_kernel(tc, x_crop, W_r, W_i, b_r, b_i, out):
                                 bank[:, c, u, :], words[:, half * HALF + c, u, :], identity[:]
                             )
                     start = (part * 2 + half) * bank_cols
-                    pairs = x_grouped[:, start : start + bank_cols].bitcast(F32)
+                    pairs = x_grouped[n][:, start : start + bank_cols].bitcast(F32)
                     nc.scalar.copy(
                         out=pairs.rearrange("p (c b u) -> p c b u", c=HALF, u=2),
                         in_=bank[:].rearrange("p c u b -> p c b u"),
                     )
-            return x_grouped
 
-        def quantise_x(n, x_grouped):
+        def quantise_x(n):
             x_codes[n] = work.tile([P, 2 * PASSES * X_COLS], U32, name="x_codes", align_bytes=64)
             x_scales[n] = work.tile([P, 2 * PASSES * X_COLS], U8, name="x_scales", align_bytes=64)
             nc.vector.quantize_mx(
-                out=x_codes[n][:].bitcast(FP8X4), scales=x_scales[n][:], in_=x_grouped[:]
+                out=x_codes[n][:].bitcast(FP8X4), scales=x_scales[n][:], in_=x_grouped[n][:]
             )
 
         def regroup_w(n):
@@ -107,11 +110,10 @@ def tile_dot_pa_k_kernel(tc, x_crop, W_r, W_i, b_r, b_i, out):
                     src.rearrange("p c (j g i) -> p c g j i", j=PACK, i=4),
                 )
 
-            first, second = slice(0, HALF), slice(HALF, PASSES)
-            for part, passes in ((REAL, first), (IMAG, first), (REAL, second)):
+            for part, passes in ((REAL, slice(0, HALF)), (IMAG, slice(0, 1)), (REAL, slice(HALF, PASSES))):
                 dst, src = views(part, passes)
                 nc.vector.tensor_copy(out=dst, in_=src)
-            for c in range(HALF, PASSES):
+            for c in range(1, PASSES):
                 dst, src = views(IMAG, slice(c, c + 1))
                 nc.scalar.copy(out=dst[:, 0], in_=src[:, 0])
             return w_grouped
@@ -161,9 +163,10 @@ def tile_dot_pa_k_kernel(tc, x_crop, W_r, W_i, b_r, b_i, out):
             nc.vector.tensor_scalar_max(out=result[:], in0=result[:], scalar1=0.0)
             nc.sync.dma_start(out=out[:, :, h, w, :], in_=result[:])
 
-        load_x(0)
-        for n in range(RAW_BUFS - 1):
-            load_x(n + 1)
+        for n in range(X_AHEAD):
+            load_x(n)
+        for n in range(RAW_BUFS - X_AHEAD):
+            load_x(n + X_AHEAD)
             load_w(n)
 
         identity = const.tile([P, P], F32)
@@ -175,8 +178,9 @@ def tile_dot_pa_k_kernel(tc, x_crop, W_r, W_i, b_r, b_i, out):
         nc.scalar.dma_start(out=bias_row[0:1, REAL, :], in_=b_r.rearrange("(o f) -> o f", o=1))
         nc.scalar.dma_start(out=bias_row[0:1, IMAG, :], in_=b_i.rearrange("(o f) -> o f", o=1))
 
-        x_grouped = transpose_x(0)
-        quantise_x(0, x_grouped)
+        for n in range(X_AHEAD):
+            transpose_x(n)
+        quantise_x(0)
 
         bias_bank = psum_t.tile([P, 2, FEATURES], F32, name="bias_bank", tag="bank")
         bias = const.tile([P, 2, FEATURES], F32)
@@ -192,15 +196,15 @@ def tile_dot_pa_k_kernel(tc, x_crop, W_r, W_i, b_r, b_i, out):
         for n in range(CHUNKS):
             if n + RAW_BUFS < CHUNKS:
                 load_x(n + RAW_BUFS)
-            if n + RAW_BUFS - 1 < CHUNKS:
-                load_w(n + RAW_BUFS - 1)
-            if n + 1 < CHUNKS:
-                x_grouped = transpose_x(n + 1)
+            if n + RAW_BUFS - X_AHEAD < CHUNKS:
+                load_w(n + RAW_BUFS - X_AHEAD)
+            if n + X_AHEAD < CHUNKS:
+                transpose_x(n + X_AHEAD)
             if n > 0 and n % CHUNKS_PER_PIXEL == 0:
                 finish_pixel(n // CHUNKS_PER_PIXEL - 1)
             w_grouped = regroup_w(n)
             if n + 1 < CHUNKS:
-                quantise_x(n + 1, x_grouped)
+                quantise_x(n + 1)
             quantise_w(n, w_grouped)
             multiply(n)
         finish_pixel(PIXELS - 1)

@@ -110,7 +110,8 @@ def tile_dot_pa_k_kernel(tc, x_crop, W_r, W_i, b_r, b_i, out):
                     src.rearrange("p c (j g i) -> p c g j i", j=PACK, i=4),
                 )
 
-            for part, passes in ((REAL, slice(0, HALF)), (IMAG, slice(0, 1)), (REAL, slice(HALF, PASSES))):
+            vector_share = ((REAL, slice(0, HALF)), (IMAG, slice(0, 1)), (REAL, slice(HALF, PASSES)))
+            for part, passes in vector_share:
                 dst, src = views(part, passes)
                 nc.vector.tensor_copy(out=dst, in_=src)
             for c in range(1, PASSES):
@@ -198,11 +199,11 @@ def tile_dot_pa_k_kernel(tc, x_crop, W_r, W_i, b_r, b_i, out):
                 load_x(n + RAW_BUFS)
             if n + RAW_BUFS - X_AHEAD < CHUNKS:
                 load_w(n + RAW_BUFS - X_AHEAD)
+            w_grouped = regroup_w(n)
             if n + X_AHEAD < CHUNKS:
                 transpose_x(n + X_AHEAD)
             if n > 0 and n % CHUNKS_PER_PIXEL == 0:
                 finish_pixel(n // CHUNKS_PER_PIXEL - 1)
-            w_grouped = regroup_w(n)
             if n + 1 < CHUNKS:
                 quantise_x(n + 1)
             quantise_w(n, w_grouped)

@@ -54,21 +54,25 @@ def tile_dot_pa_k_kernel(tc, x_crop, W_r, W_i, b_r, b_i, out):
         def place(n):
             pixel, quarter = divmod(n, CHUNKS_PER_PIXEL)
             h, w = divmod(pixel, PIXEL_COLS)
-            return h, w, slice(quarter * K_CHUNK, (quarter + 1) * K_CHUNK)
+            return h, w, quarter * K_CHUNK
 
         def load_x(n):
-            h, w, channels = place(n)
+            h, w, first = place(n)
             x_raw[n] = raw.tile([P, 2, K_CHUNK], BF16, name="x_raw", tag="x_raw")
-            nc.sync.dma_start(out=x_raw[n][:], in_=x_crop[:, :, h, w, channels])
+            nc.sync.dma_start(out=x_raw[n][:], in_=x_crop[:, :, h, w, first : first + K_CHUNK])
 
         def load_w(n):
-            h, w, channels = place(n)
+            h, w, first = place(n)
             w_raw[n] = raw.tile([P, 2, PASSES, PACK * FEATURES], BF16, name="w_raw", tag="w_raw")
-            for part, weights in ((REAL, W_r), (IMAG, W_i)):
-                nc.sync.dma_start(
-                    out=w_raw[n][:, part],
-                    in_=weights[h, w, channels, :].rearrange("(c p j) f -> p c (j f)", p=P, j=PACK),
-                )
+            for half in range(2):
+                passes = slice(half * HALF, (half + 1) * HALF)
+                top = first + half * HALF * K_PASS
+                for part, weights in ((REAL, W_r), (IMAG, W_i)):
+                    rows = weights[h, w, top : top + HALF * K_PASS, :]
+                    nc.sync.dma_start(
+                        out=w_raw[n][:, part, passes, :],
+                        in_=rows.rearrange("(c p j) f -> p c (j f)", p=P, j=PACK),
+                    )
 
         def transpose_x(n):
             x_grouped[n] = work.tile(

@@ -31,6 +31,7 @@ W_COLS = 2 * FEATURES
 
 RAW_BUFS = 6
 X_AHEAD = 2
+WORK_BUFS = 3
 
 FLOPS = 4 * PIXELS * 2 * BATCH * CHANNELS * FEATURES
 
@@ -40,7 +41,7 @@ def tile_dot_pa_k_kernel(tc, x_crop, W_r, W_i, b_r, b_i, out):
     with ExitStack() as ctx:
         const = ctx.enter_context(tc.tile_pool(name="const", bufs=1))
         raw = ctx.enter_context(tc.tile_pool(name="raw", bufs=RAW_BUFS))
-        work = ctx.enter_context(tc.tile_pool(name="work", bufs=2))
+        work = ctx.enter_context(tc.tile_pool(name="work", bufs=WORK_BUFS))
         psum_t = ctx.enter_context(tc.psum_pool(name="psum_t", bufs=4))
         psum_acc = ctx.enter_context(tc.psum_pool(name="psum_acc", bufs=2))
         ctx.enter_context(tc.manual_schedule())
@@ -54,25 +55,21 @@ def tile_dot_pa_k_kernel(tc, x_crop, W_r, W_i, b_r, b_i, out):
         def place(n):
             pixel, quarter = divmod(n, CHUNKS_PER_PIXEL)
             h, w = divmod(pixel, PIXEL_COLS)
-            return h, w, quarter * K_CHUNK
+            return h, w, slice(quarter * K_CHUNK, (quarter + 1) * K_CHUNK)
 
         def load_x(n):
-            h, w, first = place(n)
+            h, w, channels = place(n)
             x_raw[n] = raw.tile([P, 2, K_CHUNK], BF16, name="x_raw", tag="x_raw")
-            nc.sync.dma_start(out=x_raw[n][:], in_=x_crop[:, :, h, w, first : first + K_CHUNK])
+            nc.sync.dma_start(out=x_raw[n][:], in_=x_crop[:, :, h, w, channels])
 
         def load_w(n):
-            h, w, first = place(n)
+            h, w, channels = place(n)
             w_raw[n] = raw.tile([P, 2, PASSES, PACK * FEATURES], BF16, name="w_raw", tag="w_raw")
-            for half in range(2):
-                passes = slice(half * HALF, (half + 1) * HALF)
-                top = first + half * HALF * K_PASS
-                for part, weights in ((REAL, W_r), (IMAG, W_i)):
-                    rows = weights[h, w, top : top + HALF * K_PASS, :]
-                    nc.sync.dma_start(
-                        out=w_raw[n][:, part, passes, :],
-                        in_=rows.rearrange("(c p j) f -> p c (j f)", p=P, j=PACK),
-                    )
+            for part, weights in ((REAL, W_r), (IMAG, W_i)):
+                nc.sync.dma_start(
+                    out=w_raw[n][:, part],
+                    in_=weights[h, w, channels, :].rearrange("(c p j) f -> p c (j f)", p=P, j=PACK),
+                )
 
         def transpose_x(n):
             x_grouped[n] = work.tile(

@@ -8,6 +8,7 @@ F32 = mybir.dt.float32
 U32 = mybir.dt.uint32
 U8 = mybir.dt.uint8
 FP8X4 = mybir.dt.float8_e4m3fn_x4
+RELU = mybir.ActivationFunctionType.Relu
 
 P = 128
 PACK = 4
@@ -29,8 +30,9 @@ HALF = PASSES // 2
 X_COLS = BATCH
 W_COLS = 2 * FEATURES
 
+BIAS_ROUND = 1
 RAW_BUFS = 6
-X_AHEAD = 2
+X_AHEAD = 1
 WORK_BUFS = 3
 
 FLOPS = 4 * PIXELS * 2 * BATCH * CHANNELS * FEATURES
@@ -57,6 +59,13 @@ def tile_dot_pa_k_kernel(tc, x_crop, W_r, W_i, b_r, b_i, out):
             h, w = divmod(pixel, PIXEL_COLS)
             return h, w, slice(quarter * K_CHUNK, (quarter + 1) * K_CHUNK)
 
+        def load_pieces(n):
+            if n == 0:
+                return (slice(0, HALF), slice(HALF, PASSES))
+            if n == CHUNKS - 1:
+                return (slice(0, 2), slice(2, 3), slice(3, 4))
+            return (slice(0, PASSES),)
+
         def load_x(n):
             h, w, channels = place(n)
             x_raw[n] = raw.tile([P, 2, K_CHUNK], BF16, name="x_raw", tag="x_raw")
@@ -65,11 +74,10 @@ def tile_dot_pa_k_kernel(tc, x_crop, W_r, W_i, b_r, b_i, out):
         def load_w(n):
             h, w, channels = place(n)
             w_raw[n] = raw.tile([P, 2, PASSES, PACK * FEATURES], BF16, name="w_raw", tag="w_raw")
-            for part, weights in ((REAL, W_r), (IMAG, W_i)):
-                nc.sync.dma_start(
-                    out=w_raw[n][:, part],
-                    in_=weights[h, w, channels, :].rearrange("(c p j) f -> p c (j f)", p=P, j=PACK),
-                )
+            for passes in load_pieces(n):
+                for part, weights in ((REAL, W_r), (IMAG, W_i)):
+                    rows = weights[h, w, channels, :].rearrange("(c p j) f -> p c (j f)", p=P, j=PACK)
+                    nc.sync.dma_start(out=w_raw[n][:, part, passes], in_=rows[:, passes])
 
         def transpose_x(n):
             x_grouped[n] = work.tile(
@@ -100,48 +108,46 @@ def tile_dot_pa_k_kernel(tc, x_crop, W_r, W_i, b_r, b_i, out):
                 out=x_codes[n][:].bitcast(FP8X4), scales=x_scales[n][:], in_=x_grouped[n][:]
             )
 
+        def w_views(n, w_grouped, part, passes):
+            src = w_raw[n][:, part, passes, :]
+            dst = w_grouped[:, passes, part, :, :]
+            return (
+                dst.rearrange("p c (g i) j -> p c g j i", i=4),
+                src.rearrange("p c (j g i) -> p c g j i", j=PACK, i=4),
+            )
+
         def regroup_w(n):
             w_grouped = work.tile([P, PASSES, 2, FEATURES, PACK], BF16, align_bytes=64)
-
-            def views(part, passes):
-                src = w_raw[n][:, part, passes, :]
-                dst = w_grouped[:, passes, part, :, :]
-                return (
-                    dst.rearrange("p c (g i) j -> p c g j i", i=4),
-                    src.rearrange("p c (j g i) -> p c g j i", j=PACK, i=4),
-                )
-
-            vector_share = ((REAL, slice(0, HALF)), (IMAG, slice(0, 1)), (REAL, slice(HALF, PASSES)))
+            vector_share = ((REAL, slice(0, PASSES)), (IMAG, slice(0, 1)))
             for part, passes in vector_share:
-                dst, src = views(part, passes)
+                dst, src = w_views(n, w_grouped, part, passes)
                 nc.vector.tensor_copy(out=dst, in_=src)
             for c in range(1, PASSES):
-                dst, src = views(IMAG, slice(c, c + 1))
+                dst, src = w_views(n, w_grouped, IMAG, slice(c, c + 1))
                 nc.scalar.copy(out=dst[:, 0], in_=src[:, 0])
             return w_grouped
 
-        def quantise_w(n, w_grouped):
-            w_codes[n] = work.tile([P, PASSES * W_COLS], U32, name="w_codes", align_bytes=64)
-            w_scales[n] = work.tile([P, PASSES * W_COLS], U8, name="w_scales", align_bytes=64)
-            for half in range(2):
-                cols = slice(half * HALF * W_COLS, (half + 1) * HALF * W_COLS)
-                passes = slice(half * HALF, (half + 1) * HALF)
-                nc.vector.quantize_mx(
-                    out=w_codes[n][:, cols].bitcast(FP8X4),
-                    scales=w_scales[n][:, cols],
-                    in_=w_grouped[:, passes].rearrange("p c z f j -> p (c z f j)"),
-                )
+        def quantise_w(n, w_grouped, passes=slice(0, PASSES)):
+            if passes.start == 0:
+                w_codes[n] = work.tile([P, PASSES * W_COLS], U32, name="w_codes", align_bytes=64)
+                w_scales[n] = work.tile([P, PASSES * W_COLS], U8, name="w_scales", align_bytes=64)
+            cols = slice(passes.start * W_COLS, passes.stop * W_COLS)
+            nc.vector.quantize_mx(
+                out=w_codes[n][:, cols].bitcast(FP8X4),
+                scales=w_scales[n][:, cols],
+                in_=w_grouped[:, passes].rearrange("p c z f j -> p (c z f j)"),
+            )
 
-        def multiply(n):
+        def multiply(n, pieces=(slice(0, PASSES),)):
             pixel, quarter = divmod(n, CHUNKS_PER_PIXEL)
             if quarter == 0:
                 sums[pixel] = (
                     psum_acc.tile([P, 2, FEATURES], F32, name="sum_xr", tag="sum_xr"),
                     psum_acc.tile([P, 2, FEATURES], F32, name="sum_xi", tag="sum_xi"),
                 )
-            for half in range(2):
+            for passes in pieces:
                 for part in (IMAG, REAL):
-                    for c in range(half * HALF, (half + 1) * HALF):
+                    for c in range(passes.start, passes.stop):
                         x_cols = slice((part * PASSES + c) * X_COLS, (part * PASSES + c + 1) * X_COLS)
                         w_cols = slice(c * W_COLS, (c + 1) * W_COLS)
                         nc.tensor.matmul_mx(
@@ -161,15 +167,20 @@ def tile_dot_pa_k_kernel(tc, x_crop, W_r, W_i, b_r, b_i, out):
             result = work.tile([P, 2, FEATURES], F32)
             nc.vector.tensor_sub(out=rest[:, REAL, :], in0=bias[:, REAL, :], in1=sum_xi[:, IMAG, :])
             nc.vector.tensor_add(out=rest[:, IMAG, :], in0=bias[:, IMAG, :], in1=sum_xi[:, REAL, :])
-            nc.vector.tensor_add(out=result[:], in0=rest[:], in1=sum_xr[:])
-            nc.vector.tensor_scalar_max(out=result[:], in0=result[:], scalar1=0.0)
-            nc.sync.dma_start(out=out[:, :, h, w, :], in_=result[:])
+            for part in (REAL, IMAG):
+                nc.vector.tensor_add(out=rest[:, part, :], in0=rest[:, part, :], in1=sum_xr[:, part, :])
+            for part in (REAL, IMAG):
+                nc.scalar.activation(out=result[:, part, :], in_=rest[:, part, :], func=RELU)
+                nc.sync.dma_start(out=out[:, part, h, w, :], in_=result[:, part, :])
 
-        for n in range(X_AHEAD):
+        load_w(0)
+        load_x(0)
+        load_w(1)
+        load_x(1)
+        for n in range(2, RAW_BUFS - 1):
             load_x(n)
-        for n in range(RAW_BUFS - X_AHEAD):
-            load_x(n + X_AHEAD)
             load_w(n)
+        load_x(RAW_BUFS - 1)
 
         identity = const.tile([P, P], F32)
         make_identity(nc, identity[:])
@@ -177,36 +188,50 @@ def tile_dot_pa_k_kernel(tc, x_crop, W_r, W_i, b_r, b_i, out):
         bias_row = const.tile([P, 2, FEATURES], BF16)
         nc.vector.memset(ones[:], 1.0)
         nc.vector.memset(bias_row[:], 0.0)
-        nc.scalar.dma_start(out=bias_row[0:1, REAL, :], in_=b_r.rearrange("(o f) -> o f", o=1))
-        nc.scalar.dma_start(out=bias_row[0:1, IMAG, :], in_=b_i.rearrange("(o f) -> o f", o=1))
+        nc.gpsimd.dma_start(out=bias_row[0:1, REAL, :], in_=b_r.rearrange("(o f) -> o f", o=1))
+        nc.gpsimd.dma_start(out=bias_row[0:1, IMAG, :], in_=b_i.rearrange("(o f) -> o f", o=1))
 
-        for n in range(X_AHEAD):
-            transpose_x(n)
-        quantise_x(0)
+        w_grouped = regroup_w(0)
+        quantise_w(0, w_grouped)
+        transpose_x(0)
+        w_grouped = regroup_w(1)
 
-        bias_bank = psum_t.tile([P, 2, FEATURES], F32, name="bias_bank", tag="bank")
-        bias = const.tile([P, 2, FEATURES], F32)
-        nc.tensor.matmul(
-            out=bias_bank[:].rearrange("b z f -> b (z f)"),
-            lhsT=ones[:],
-            rhs=bias_row[:].rearrange("k z f -> k (z f)"),
-            start=True,
-            stop=True,
-        )
-        nc.scalar.copy(out=bias[:], in_=bias_bank[:])
-
-        for n in range(CHUNKS):
+        for n in range(CHUNKS - 1):
             if n + RAW_BUFS < CHUNKS:
                 load_x(n + RAW_BUFS)
-            if n + RAW_BUFS - X_AHEAD < CHUNKS:
-                load_w(n + RAW_BUFS - X_AHEAD)
-            w_grouped = regroup_w(n)
+            if n + RAW_BUFS - 1 < CHUNKS:
+                load_w(n + RAW_BUFS - 1)
+            if n > 1:
+                w_grouped = regroup_w(n)
             if n + X_AHEAD < CHUNKS:
                 transpose_x(n + X_AHEAD)
             if n > 0 and n % CHUNKS_PER_PIXEL == 0:
                 finish_pixel(n // CHUNKS_PER_PIXEL - 1)
-            if n + 1 < CHUNKS:
-                quantise_x(n + 1)
-            quantise_w(n, w_grouped)
+            quantise_x(n)
+            if n > 0:
+                quantise_w(n, w_grouped)
             multiply(n)
+            if n == BIAS_ROUND:
+                bias_bank = psum_t.tile([P, 2, FEATURES], F32, name="bias_bank", tag="bank")
+                bias = const.tile([P, 2, FEATURES], F32)
+                nc.tensor.matmul(
+                    out=bias_bank[:].rearrange("b z f -> b (z f)"),
+                    lhsT=ones[:],
+                    rhs=bias_row[:].rearrange("k z f -> k (z f)"),
+                    start=True,
+                    stop=True,
+                )
+                nc.scalar.copy(out=bias[:], in_=bias_bank[:])
+
+        n = CHUNKS - 1
+        quantise_x(n)
+        w_grouped = work.tile([P, PASSES, 2, FEATURES, PACK], BF16, align_bytes=64)
+        for passes in load_pieces(n):
+            dst, src = w_views(n, w_grouped, REAL, passes)
+            nc.vector.tensor_copy(out=dst, in_=src)
+            for c in range(passes.start, passes.stop):
+                dst, src = w_views(n, w_grouped, IMAG, slice(c, c + 1))
+                nc.scalar.copy(out=dst[:, 0], in_=src[:, 0])
+            quantise_w(n, w_grouped, passes)
+            multiply(n, (passes,))
         finish_pixel(PIXELS - 1)

@@ -32,7 +32,7 @@ W_COLS = 2 * FEATURES
 
 BIAS_ROUND = 1
 RAW_BUFS = 6
-X_AHEAD = 1
+X_AHEAD = 2
 WORK_BUFS = 3
 
 FLOPS = 4 * PIXELS * 2 * BATCH * CHANNELS * FEATURES
@@ -177,10 +177,10 @@ def tile_dot_pa_k_kernel(tc, x_crop, W_r, W_i, b_r, b_i, out):
         load_x(0)
         load_w(1)
         load_x(1)
+        load_x(2)
         for n in range(2, RAW_BUFS - 1):
-            load_x(n)
+            load_x(n + 1)
             load_w(n)
-        load_x(RAW_BUFS - 1)
 
         identity = const.tile([P, P], F32)
         make_identity(nc, identity[:])
@@ -195,6 +195,8 @@ def tile_dot_pa_k_kernel(tc, x_crop, W_r, W_i, b_r, b_i, out):
         quantise_w(0, w_grouped)
         transpose_x(0)
         w_grouped = regroup_w(1)
+        quantise_x(0)
+        transpose_x(1)
 
         for n in range(CHUNKS - 1):
             if n + RAW_BUFS < CHUNKS:
@@ -207,7 +209,7 @@ def tile_dot_pa_k_kernel(tc, x_crop, W_r, W_i, b_r, b_i, out):
                 transpose_x(n + X_AHEAD)
             if n > 0 and n % CHUNKS_PER_PIXEL == 0:
                 finish_pixel(n // CHUNKS_PER_PIXEL - 1)
-            quantise_x(n)
+            quantise_x(n + 1)
             if n > 0:
                 quantise_w(n, w_grouped)
             multiply(n)
@@ -224,7 +226,6 @@ def tile_dot_pa_k_kernel(tc, x_crop, W_r, W_i, b_r, b_i, out):
                 nc.scalar.copy(out=bias[:], in_=bias_bank[:])
 
         n = CHUNKS - 1
-        quantise_x(n)
         w_grouped = work.tile([P, PASSES, 2, FEATURES, PACK], BF16, align_bytes=64)
         for passes in load_pieces(n):
             dst, src = w_views(n, w_grouped, REAL, passes)

@@ -33,6 +33,7 @@ W_COLS = 2 * FEATURES
 BIAS_ROUND = 1
 RAW_BUFS = 6
 X_AHEAD = 2
+CODE_BUFS = 4
 WORK_BUFS = 3
 
 FLOPS = 4 * PIXELS * 2 * BATCH * CHANNELS * FEATURES
@@ -102,8 +103,8 @@ def tile_dot_pa_k_kernel(tc, x_crop, W_r, W_i, b_r, b_i, out):
                     )
 
         def quantise_x(n):
-            x_codes[n] = work.tile([P, 2 * PASSES * X_COLS], U32, name="x_codes", align_bytes=64)
-            x_scales[n] = work.tile([P, 2 * PASSES * X_COLS], U8, name="x_scales", align_bytes=64)
+            x_codes[n] = work.tile([P, 2 * PASSES * X_COLS], U32, name="x_codes", align_bytes=64, bufs=CODE_BUFS)
+            x_scales[n] = work.tile([P, 2 * PASSES * X_COLS], U8, name="x_scales", align_bytes=64, bufs=CODE_BUFS)
             nc.vector.quantize_mx(
                 out=x_codes[n][:].bitcast(FP8X4), scales=x_scales[n][:], in_=x_grouped[n][:]
             )
@@ -129,8 +130,8 @@ def tile_dot_pa_k_kernel(tc, x_crop, W_r, W_i, b_r, b_i, out):
 
         def quantise_w(n, w_grouped, passes=slice(0, PASSES)):
             if passes.start == 0:
-                w_codes[n] = work.tile([P, PASSES * W_COLS], U32, name="w_codes", align_bytes=64)
-                w_scales[n] = work.tile([P, PASSES * W_COLS], U8, name="w_scales", align_bytes=64)
+                w_codes[n] = work.tile([P, PASSES * W_COLS], U32, name="w_codes", align_bytes=64, bufs=CODE_BUFS)
+                w_scales[n] = work.tile([P, PASSES * W_COLS], U8, name="w_scales", align_bytes=64, bufs=CODE_BUFS)
             cols = slice(passes.start * W_COLS, passes.stop * W_COLS)
             nc.vector.quantize_mx(
                 out=w_codes[n][:, cols].bitcast(FP8X4),
@@ -207,12 +208,13 @@ def tile_dot_pa_k_kernel(tc, x_crop, W_r, W_i, b_r, b_i, out):
                 w_grouped = regroup_w(n)
             if n + X_AHEAD < CHUNKS:
                 transpose_x(n + X_AHEAD)
-            if n > 0 and n % CHUNKS_PER_PIXEL == 0:
+            if n > 0:
+                multiply(n - 1)
+            if n > 1 and n % CHUNKS_PER_PIXEL == 1:
                 finish_pixel(n // CHUNKS_PER_PIXEL - 1)
             quantise_x(n + 1)
             if n > 0:
                 quantise_w(n, w_grouped)
-            multiply(n)
             if n == BIAS_ROUND:
                 bias_bank = psum_t.tile([P, 2, FEATURES], F32, name="bias_bank", tag="bank")
                 bias = const.tile([P, 2, FEATURES], F32)
@@ -226,6 +228,7 @@ def tile_dot_pa_k_kernel(tc, x_crop, W_r, W_i, b_r, b_i, out):
                 nc.scalar.copy(out=bias[:], in_=bias_bank[:])
 
         n = CHUNKS - 1
+        multiply(n - 1)
         w_grouped = work.tile([P, PASSES, 2, FEATURES, PACK], BF16, align_bytes=64)
         for passes in load_pieces(n):
             dst, src = w_views(n, w_grouped, REAL, passes)

@@ -26,6 +26,7 @@ K_CHUNK = PASSES * K_PASS
 CHUNKS_PER_PIXEL = CHANNELS // K_CHUNK
 CHUNKS = PIXELS * CHUNKS_PER_PIXEL
 HALF = PASSES // 2
+HALVES = (slice(0, HALF), slice(HALF, PASSES))
 
 X_COLS = BATCH
 W_COLS = 2 * FEATURES
@@ -61,16 +62,15 @@ def tile_dot_pa_k_kernel(tc, x_crop, W_r, W_i, b_r, b_i, out):
             return h, w, slice(quarter * K_CHUNK, (quarter + 1) * K_CHUNK)
 
         def load_pieces(n):
-            if n == 0:
-                return (slice(0, HALF), slice(HALF, PASSES))
-            if n == CHUNKS - 1:
-                return (slice(0, 2), slice(2, 3), slice(3, 4))
+            if n == 0 or n >= CHUNKS - 2:
+                return HALVES
             return (slice(0, PASSES),)
 
         def load_x(n):
             h, w, channels = place(n)
             x_raw[n] = raw.tile([P, 2, K_CHUNK], BF16, name="x_raw", tag="x_raw")
-            nc.sync.dma_start(out=x_raw[n][:], in_=x_crop[:, :, h, w, channels])
+            for parts in (slice(0, 1), slice(1, 2)) if n == 0 else (slice(0, 2),):
+                nc.sync.dma_start(out=x_raw[n][:, parts], in_=x_crop[:, parts, h, w, channels])
 
         def load_w(n):
             h, w, channels = place(n)
@@ -119,13 +119,14 @@ def tile_dot_pa_k_kernel(tc, x_crop, W_r, W_i, b_r, b_i, out):
 
         def regroup_w(n):
             w_grouped = work.tile([P, PASSES, 2, FEATURES, PACK], BF16, align_bytes=64)
-            vector_share = ((REAL, slice(0, PASSES)), (IMAG, slice(0, 1)))
-            for part, passes in vector_share:
-                dst, src = w_views(n, w_grouped, part, passes)
+            for half in load_pieces(n):
+                dst, src = w_views(n, w_grouped, REAL, half)
                 nc.vector.tensor_copy(out=dst, in_=src)
-            for c in range(1, PASSES):
-                dst, src = w_views(n, w_grouped, IMAG, slice(c, c + 1))
-                nc.scalar.copy(out=dst[:, 0], in_=src[:, 0])
+                if half.start == 0:
+                    dst, src = w_views(n, w_grouped, IMAG, slice(0, 1))
+                    nc.vector.tensor_copy(out=dst, in_=src)
+                dst, src = w_views(n, w_grouped, IMAG, slice(max(1, half.start), half.stop))
+                nc.scalar.copy(out=dst, in_=src)
             return w_grouped
 
         def quantise_w(n, w_grouped, passes=slice(0, PASSES)):
@@ -214,7 +215,8 @@ def tile_dot_pa_k_kernel(tc, x_crop, W_r, W_i, b_r, b_i, out):
                 finish_pixel(n // CHUNKS_PER_PIXEL - 1)
             quantise_x(n + 1)
             if n > 0:
-                quantise_w(n, w_grouped)
+                for passes in load_pieces(n):
+                    quantise_w(n, w_grouped, passes)
             if n == BIAS_ROUND:
                 bias_bank = psum_t.tile([P, 2, FEATURES], F32, name="bias_bank", tag="bank")
                 bias = const.tile([P, 2, FEATURES], F32)
@@ -230,12 +232,12 @@ def tile_dot_pa_k_kernel(tc, x_crop, W_r, W_i, b_r, b_i, out):
         n = CHUNKS - 1
         multiply(n - 1)
         w_grouped = work.tile([P, PASSES, 2, FEATURES, PACK], BF16, align_bytes=64)
-        for passes in load_pieces(n):
+        for passes in HALVES:
             dst, src = w_views(n, w_grouped, REAL, passes)
             nc.vector.tensor_copy(out=dst, in_=src)
-            for c in range(passes.start, passes.stop):
-                dst, src = w_views(n, w_grouped, IMAG, slice(c, c + 1))
-                nc.scalar.copy(out=dst[:, 0], in_=src[:, 0])
+            dst, src = w_views(n, w_grouped, IMAG, passes)
+            nc.scalar.copy(out=dst, in_=src)
+        for passes in HALVES:
             quantise_w(n, w_grouped, passes)
             multiply(n, (passes,))
         finish_pixel(PIXELS - 1)

from contextlib import ExitStack

import concourse.mybir as mybir
from concourse.masks import make_identity

BF16 = mybir.dt.bfloat16
F32 = mybir.dt.float32
U32 = mybir.dt.uint32
U8 = mybir.dt.uint8
FP8X4 = mybir.dt.float8_e4m3fn_x4
RELU = mybir.ActivationFunctionType.Relu

P = 128
PACK = 4
K_PASS = P * PACK

BATCH = 128
PIXEL_COLS = 2
PIXELS = 4
CHANNELS = 8192
FEATURES = 128
REAL, IMAG = 0, 1

PASSES = 4
K_CHUNK = PASSES * K_PASS
CHUNKS_PER_PIXEL = CHANNELS // K_CHUNK
CHUNKS = PIXELS * CHUNKS_PER_PIXEL
HALF = PASSES // 2
HALVES = (slice(0, HALF), slice(HALF, PASSES))

X_COLS = BATCH
W_COLS = 2 * FEATURES

BIAS_ROUND = 1
RAW_BUFS = 6
X_AHEAD = 2
CODE_BUFS = 4
WORK_BUFS = 3

FLOPS = 4 * PIXELS * 2 * BATCH * CHANNELS * FEATURES


def tile_dot_pa_k_kernel(tc, x_crop, W_r, W_i, b_r, b_i, out):
    nc = tc.nc
    with ExitStack() as ctx:
        const = ctx.enter_context(tc.tile_pool(name="const", bufs=1))
        raw = ctx.enter_context(tc.tile_pool(name="raw", bufs=RAW_BUFS))
        work = ctx.enter_context(tc.tile_pool(name="work", bufs=WORK_BUFS))
        psum_t = ctx.enter_context(tc.psum_pool(name="psum_t", bufs=4))
        psum_acc = ctx.enter_context(tc.psum_pool(name="psum_acc", bufs=2))
        ctx.enter_context(tc.manual_schedule())

        x_raw, w_raw = {}, {}
        x_grouped = {}
        x_codes, x_scales = {}, {}
        w_codes, w_scales = {}, {}
        sums = {}

        def place(n):
            pixel, quarter = divmod(n, CHUNKS_PER_PIXEL)
            h, w = divmod(pixel, PIXEL_COLS)
            return h, w, slice(quarter * K_CHUNK, (quarter + 1) * K_CHUNK)

        def load_pieces(n):
            if n == 0 or n >= CHUNKS - 2:
                return HALVES
            return (slice(0, PASSES),)

        def load_x(n):
            h, w, channels = place(n)
            x_raw[n] = raw.tile([P, 2, K_CHUNK], BF16, name="x_raw", tag="x_raw")
            for parts in (slice(0, 1), slice(1, 2)) if n == 0 else (slice(0, 2),):
                nc.sync.dma_start(out=x_raw[n][:, parts], in_=x_crop[:, parts, h, w, channels])

        def load_w(n):
            h, w, channels = place(n)
            w_raw[n] = raw.tile([P, 2, PASSES, PACK * FEATURES], BF16, name="w_raw", tag="w_raw")
            for passes in load_pieces(n):
                for part, weights in ((REAL, W_r), (IMAG, W_i)):
                    rows = weights[h, w, channels, :].rearrange("(c p j) f -> p c (j f)", p=P, j=PACK)
                    nc.sync.dma_start(out=w_raw[n][:, part, passes], in_=rows[:, passes])

        def transpose_x(n):
            x_grouped[n] = work.tile(
                [P, 2 * PASSES * X_COLS * PACK], BF16, name="x_grouped", align_bytes=64
            )
            bank_cols = HALF * X_COLS * PACK
            for part in (REAL, IMAG):
                words = x_raw[n][:, part, :].bitcast(F32)
                words = words.rearrange("b (c p u) -> b c u p", p=P, u=2)
                for half in range(2):
                    bank = psum_t.tile([P, HALF, 2, BATCH], F32, name="bank", tag="bank")
                    for c in range(HALF):
                        for u in range(2):
                            nc.tensor.transpose(
                                bank[:, c, u, :], words[:, half * HALF + c, u, :], identity[:]
                            )
                    start = (part * 2 + half) * bank_cols
                    pairs = x_grouped[n][:, start : start + bank_cols].bitcast(F32)
                    nc.scalar.copy(
                        out=pairs.rearrange("p (c b u) -> p c b u", c=HALF, u=2),
                        in_=bank[:].rearrange("p c u b -> p c b u"),
                    )

        def quantise_x(n):
            x_codes[n] = work.tile([P, 2 * PASSES * X_COLS], U32, name="x_codes", align_bytes=64, bufs=CODE_BUFS)
            x_scales[n] = work.tile([P, 2 * PASSES * X_COLS], U8, name="x_scales", align_bytes=64, bufs=CODE_BUFS)
            nc.vector.quantize_mx(
                out=x_codes[n][:].bitcast(FP8X4), scales=x_scales[n][:], in_=x_grouped[n][:]
            )

        def w_views(n, w_grouped, part, passes):
            src = w_raw[n][:, part, passes, :]
            dst = w_grouped[:, passes, part, :, :]
            return (
                dst.rearrange("p c (g i) j -> p c g j i", i=4),
                src.rearrange("p c (j g i) -> p c g j i", j=PACK, i=4),
            )

        def regroup_w(n):
            w_grouped = work.tile([P, PASSES, 2, FEATURES, PACK], BF16, align_bytes=64)
            for half in load_pieces(n):
                dst, src = w_views(n, w_grouped, REAL, half)
                nc.vector.tensor_copy(out=dst, in_=src)
                if half.start == 0:
                    dst, src = w_views(n, w_grouped, IMAG, slice(0, 1))
                    nc.vector.tensor_copy(out=dst, in_=src)
                dst, src = w_views(n, w_grouped, IMAG, slice(max(1, half.start), half.stop))
                nc.scalar.copy(out=dst, in_=src)
            return w_grouped

        def quantise_w(n, w_grouped, passes=slice(0, PASSES)):
            if passes.start == 0:
                w_codes[n] = work.tile([P, PASSES * W_COLS], U32, name="w_codes", align_bytes=64, bufs=CODE_BUFS)
                w_scales[n] = work.tile([P, PASSES * W_COLS], U8, name="w_scales", align_bytes=64, bufs=CODE_BUFS)
            cols = slice(passes.start * W_COLS, passes.stop * W_COLS)
            nc.vector.quantize_mx(
                out=w_codes[n][:, cols].bitcast(FP8X4),
                scales=w_scales[n][:, cols],
                in_=w_grouped[:, passes].rearrange("p c z f j -> p (c z f j)"),
            )

        def multiply(n, pieces=(slice(0, PASSES),)):
            pixel, quarter = divmod(n, CHUNKS_PER_PIXEL)
            if quarter == 0:
                sums[pixel] = (
                    psum_acc.tile([P, 2, FEATURES], F32, name="sum_xr", tag="sum_xr"),
                    psum_acc.tile([P, 2, FEATURES], F32, name="sum_xi", tag="sum_xi"),
                )
            for passes in pieces:
                for part in (IMAG, REAL):
                    for c in range(passes.start, passes.stop):
                        x_cols = slice((part * PASSES + c) * X_COLS, (part * PASSES + c + 1) * X_COLS)
                        w_cols = slice(c * W_COLS, (c + 1) * W_COLS)
                        nc.tensor.matmul_mx(
                            out=sums[pixel][part][:].rearrange("b z f -> b (z f)"),
                            lhsT=x_codes[n][:, x_cols].bitcast(FP8X4),
                            lhsT_scale=x_scales[n][:, x_cols],
                            rhs=w_codes[n][:, w_cols].bitcast(FP8X4),
                            rhs_scale=w_scales[n][:, w_cols],
                            start=(quarter == 0 and c == 0),
                            stop=(quarter == CHUNKS_PER_PIXEL - 1 and c == PASSES - 1),
                        )

        def finish_pixel(pixel):
            h, w = divmod(pixel, PIXEL_COLS)
            sum_xr, sum_xi = sums[pixel]
            rest = work.tile([P, 2, FEATURES], F32)
            result = work.tile([P, 2, FEATURES], F32)
            nc.vector.tensor_sub(out=rest[:, REAL, :], in0=bias[:, REAL, :], in1=sum_xi[:, IMAG, :])
            nc.vector.tensor_add(out=rest[:, IMAG, :], in0=bias[:, IMAG, :], in1=sum_xi[:, REAL, :])
            for part in (REAL, IMAG):
                nc.vector.tensor_add(out=rest[:, part, :], in0=rest[:, part, :], in1=sum_xr[:, part, :])
            for part in (REAL, IMAG):
                nc.scalar.activation(out=result[:, part, :], in_=rest[:, part, :], func=RELU)
                nc.sync.dma_start(out=out[:, part, h, w, :], in_=result[:, part, :])

        load_w(0)
        load_x(0)
        load_w(1)
        load_x(1)
        load_x(2)
        for n in range(2, RAW_BUFS - 1):
            load_x(n + 1)
            load_w(n)

        identity = const.tile([P, P], F32)
        make_identity(nc, identity[:])
        ones = const.tile([P, P], BF16)
        bias_row = const.tile([P, 2, FEATURES], BF16)
        nc.vector.memset(ones[:], 1.0)
        nc.vector.memset(bias_row[:], 0.0)
        nc.gpsimd.dma_start(out=bias_row[0:1, REAL, :], in_=b_r.rearrange("(o f) -> o f", o=1))
        nc.gpsimd.dma_start(out=bias_row[0:1, IMAG, :], in_=b_i.rearrange("(o f) -> o f", o=1))

        w_grouped = regroup_w(0)
        quantise_w(0, w_grouped)
        transpose_x(0)
        w_grouped = regroup_w(1)
        quantise_x(0)
        transpose_x(1)

        for n in range(CHUNKS - 1):
            if n + RAW_BUFS < CHUNKS:
                load_x(n + RAW_BUFS)
            if n + RAW_BUFS - 1 < CHUNKS:
                load_w(n + RAW_BUFS - 1)
            if n > 1:
                w_grouped = regroup_w(n)
            if n + X_AHEAD < CHUNKS:
                transpose_x(n + X_AHEAD)
            if n > 0:
                multiply(n - 1)
            if n > 1 and n % CHUNKS_PER_PIXEL == 1:
                finish_pixel(n // CHUNKS_PER_PIXEL - 1)
            quantise_x(n + 1)
            if n > 0:
                for passes in load_pieces(n):
                    quantise_w(n, w_grouped, passes)
            if n == BIAS_ROUND:
                bias_bank = psum_t.tile([P, 2, FEATURES], F32, name="bias_bank", tag="bank")
                bias = const.tile([P, 2, FEATURES], F32)
                nc.tensor.matmul(
                    out=bias_bank[:].rearrange("b z f -> b (z f)"),
                    lhsT=ones[:],
                    rhs=bias_row[:].rearrange("k z f -> k (z f)"),
                    start=True,
                    stop=True,
                )
                nc.scalar.copy(out=bias[:], in_=bias_bank[:])

        n = CHUNKS - 1
        multiply(n - 1)
        w_grouped = work.tile([P, PASSES, 2, FEATURES, PACK], BF16, align_bytes=64)
        for passes in HALVES:
            dst, src = w_views(n, w_grouped, REAL, passes)
            nc.vector.tensor_copy(out=dst, in_=src)
            dst, src = w_views(n, w_grouped, IMAG, passes)
            nc.scalar.copy(out=dst, in_=src)
        for passes in HALVES:
            quantise_w(n, w_grouped, passes)
            multiply(n, (passes,))
        finish_pixel(PIXELS - 1)
